import numpy as np
import ml_dtypes


def mxq(x, axis, fmt="e4m3"):
    dtype, down = {"e4m3": (ml_dtypes.float8_e4m3fn, 7), "e5m2": (ml_dtypes.float8_e5m2, 14)}[fmt]
    v = np.moveaxis(np.asarray(x, np.float32).astype(ml_dtypes.bfloat16).astype(np.float64), axis, -1)
    blocks = v.reshape(v.shape[:-1] + (-1, 32))
    amax = np.abs(blocks).max(-1, keepdims=True)
    byte = np.maximum(np.where(amax > 0, np.frexp(amax)[1] - 1 + 127, 0) - down, 1)
    scale = np.exp2(byte - 127.0)
    codes = (blocks / scale).astype(np.float32).astype(dtype).astype(np.float64)
    return np.moveaxis((codes * scale).reshape(v.shape), -1, axis)


WIDE = False


def mx_kscale(k):
    if not WIDE:
        return np.ones(k)
    levels = np.array([10, -10, 5, -5, 0])
    a = np.random.permutation(np.resize(levels, k // 512 * 4)).reshape(k // 512, 4)
    idx = np.arange(k)
    return np.exp2(a[idx // 512, idx % 128 // 32])


BF16 = ml_dtypes.bfloat16


def bf(x):
    return np.asarray(x, np.float32).astype(BF16)


def f64(x):
    return np.asarray(x).astype(np.float64)


B, STACK, TUBE, CH, IMG, PATCH, EMBED = 4, 16, 2, 1, 96, 16, 1024
GH = IMG // PATCH
GW = IMG // PATCH
GD = STACK // TUBE
K = TUBE * CH * PATCH * PATCH


def _sincos_1d(dim, pos):
    omega = 1.0 / (10000.0 ** (np.arange(dim // 2, dtype=np.float64) / (dim / 2.0)))
    out = pos[:, None].astype(np.float64) * omega[None, :]
    return np.concatenate([np.sin(out), np.cos(out)], axis=1)


def get_3d_sincos_pos_embed(grid_h, grid_w, grid_depth, embed_dim):
    dim_t = embed_dim // 4
    dim_s = embed_dim - dim_t
    emb_t = _sincos_1d(dim_t, np.arange(grid_depth))
    emb_h = _sincos_1d(dim_s // 2, np.arange(grid_h))
    emb_w = _sincos_1d(dim_s - dim_s // 2, np.arange(grid_w))
    emb_hw = np.concatenate([np.repeat(emb_h, grid_w, axis=0), np.tile(emb_w, (grid_h, 1))], axis=1)
    ns = grid_h * grid_w
    return np.concatenate([np.repeat(emb_t, ns, axis=0), np.tile(emb_hw, (grid_depth, 1))], axis=1)


def setup_inputs():
    s = mx_kscale(K)
    sv = s.reshape(TUBE, CH, PATCH, PATCH)[:, :, None, :, None, :]
    video = np.random.standard_normal((B, GD, TUBE, CH, GH, PATCH, GW, PATCH)) * sv
    return {"video": bf(video.reshape(B, STACK, CH, IMG, IMG)),
            "W": bf(np.random.standard_normal((EMBED, K)) / np.sqrt(K) / s[None, :]),
            "b": bf(np.random.standard_normal(EMBED) * 0.3),
            "pos_embed": bf(get_3d_sincos_pos_embed(GH, GW, GD, EMBED)[None])}


def reference(video, W, b, pos_embed):
    video = f64(video)
    B_, T, C, H, W_ = video.shape
    p = PATCH
    gh, gw = H // p, W_ // p
    ns = gh * gw
    x = video.reshape(B_ * T, C, gh, p, gw, p)
    x = x.transpose(0, 2, 4, 1, 3, 5)
    x = x.reshape(B_, T, ns, C * p * p)
    x = x.reshape(B_, GD, TUBE, ns, C * p * p)
    x = x.transpose(0, 1, 3, 2, 4)
    tubelets = x.reshape(B_, GD * ns, TUBE * C * p * p)
    tokens = (mxq(tubelets, 2, "e4m3") @ mxq(f64(W), 1, "e4m3").T) + f64(b) + f64(pos_embed)
    return tokens

@@ -1,0 +1,147 @@
+from contextlib import ExitStack
+
+import concourse.mybir as mybir
+from concourse.masks import make_identity
+
+F32 = mybir.dt.float32
+BF16 = mybir.dt.bfloat16
+U32 = mybir.dt.uint32
+U8 = mybir.dt.uint8
+FP8X4 = mybir.dt.float8_e4m3fn_x4
+ADD = mybir.AluOpType.add
+P = 128
+FLOPS = 2 * 1152 * 512 * 1024
+
+
+def tile_tubeletembedding_kernel(tc, video, W, b, pos_embed, out):
+    nc = tc.nc
+    with ExitStack() as ctx:
+        keep = ctx.enter_context(tc.tile_pool(name="keep", bufs=1))
+        psum = ctx.enter_context(tc.psum_pool(name="psum", bufs=8))
+
+        ident = keep.tile([P, P], F32)
+        make_identity(nc, ident[:])
+        perm1 = keep.tile([P, P], F32)
+        nc.vector.tensor_copy(
+            out=perm1[:].rearrange("p (a h t) -> p a h t", h=2, t=2),
+            in_=ident[:].rearrange("p (a t h) -> p a h t", t=2, h=2),
+        )
+        ones = keep.tile([P, P], BF16)
+        nc.vector.memset(ones[:], 1.0)
+        bz = keep.tile([P, 1024], BF16)
+        nc.vector.memset(bz[:], 0.0)
+
+        vid = video.rearrange("b t o (h c y) x -> (b t o h) c (y x)", h=2, c=3, y=16)
+        wv = W.rearrange("(a p) k -> p a k", p=P)
+        pv = pos_embed.rearrange("o (s r) e -> (o s) r e", r=18)
+        v_sb = keep.tile([P, 3, 1536], BF16)
+        w_sb = keep.tile([P, 8, 512], BF16)
+        pos_sb = [keep.tile([P, 1024], BF16, name="pos%d" % g) for g in range(3)]
+        nc.sync.dma_start(out=bz[0:1, :], in_=b.unsqueeze(0))
+        nc.sync.dma_start(out=v_sb[:, 0, :], in_=vid[:, 0, :])
+        nc.sync.dma_start(out=v_sb[:, 1, :], in_=vid[:, 1, :])
+        nc.sync.dma_start(out=w_sb[:, 0:4, :], in_=wv[:, 0:4, :])
+        nc.sync.dma_start(out=pos_sb[0][:], in_=pv[:, 0:8, :])
+        nc.sync.dma_start(out=w_sb[:, 4:8, :], in_=wv[:, 4:8, :])
+        nc.sync.dma_start(out=v_sb[:, 2, :], in_=vid[:, 2, :])
+        nc.sync.dma_start(out=pos_sb[1][:], in_=pv[:, 8:16, :])
+        for bi in range(4):
+            nc.sync.dma_start(out=pos_sb[2][32 * bi:32 * (bi + 1), :], in_=pv[:, 16:18, :])
+
+        bbc = keep.tile([P, 1024], F32)
+        for h in range(2):
+            pb = psum.tile([P, 512], F32, tag="bank")
+            nc.tensor.matmul(out=pb[:], lhsT=ones[:], rhs=bz[:, h * 512:(h + 1) * 512], start=True, stop=True)
+            nc.scalar.copy(out=bbc[:, h * 512:(h + 1) * 512], in_=pb[:])
+
+        v2 = keep.tile([P, 4608], BF16)
+        v2w = v2[:].bitcast(F32)
+        grp = keep.tile([P, 4608], BF16, align_bytes=64)
+        grpw = grp[:].bitcast(F32)
+        tokc = keep.tile([P, 1152], U32, align_bytes=64)
+        toks = keep.tile([P, 1152], U8, align_bytes=64)
+        gw = keep.tile([P, 4096], BF16, align_bytes=64)
+        gww = gw[:].bitcast(F32)
+        wc = keep.tile([P, 1024], U32, align_bytes=64)
+        ws = keep.tile([P, 1024], U8, align_bytes=64)
+        w_w = w_sb[:].rearrange("p a k -> p (a k)").bitcast(F32)
+        posb = [keep.tile([P, 1024], F32, name="posb%d" % g) for g in range(3)]
+
+        def regroup(c, j0, j1):
+            nc.vector.tensor_copy(
+                out=v2[:, c * 1536 + j0 * 256:c * 1536 + j1 * 256].rearrange("p (j y x) -> p j y x", y=16, x=16),
+                in_=v_sb[:, c, :].rearrange("p (y j x) -> p j y x", j=6, x=16)[:, j0:j1, :, :],
+            )
+
+        def tok_bank(r0, n, perm, dst):
+            pt = psum.tile([P, 512], F32, tag="bank")
+            for i in range(n):
+                r = r0 + i
+                nc.tensor.transpose(pt[:, i * P:(i + 1) * P], v2w[:, r * P:(r + 1) * P], perm[:])
+            nc.scalar.copy(out=dst, in_=pt[:, 0:n * P].rearrange("p (r x t) -> p x r t", r=n, t=2))
+
+        def tok_group(g):
+            view = grpw[:, g * 1024:(g + 1) * 1024].rearrange("p (x r t) -> p x r t", r=8, t=2)
+            for q in range(2):
+                tok_bank(8 * g + 4 * q, 4, perm1, view[:, :, 4 * q:4 * q + 4, :])
+
+        def w_half(h):
+            for q in range(2):
+                a0 = 4 * h + 2 * q
+                pt = psum.tile([P, 512], F32, tag="bank")
+                for i in range(4):
+                    a, u = a0 + i // 2, i % 2
+                    nc.tensor.transpose(pt[:, i * P:(i + 1) * P], w_w[:, a * 256 + u * P:a * 256 + (u + 1) * P], ident[:])
+                nc.vector.tensor_copy(
+                    out=gww[:, a0 * 256:(a0 + 2) * 256].rearrange("p (a e u) -> p a e u", a=2, u=2),
+                    in_=pt[:].rearrange("p (a u e) -> p a e u", a=2, u=2),
+                )
+
+        def quant_tok(c0, n):
+            nc.vector.quantize_mx(out=tokc[:, c0:c0 + n].bitcast(FP8X4), scales=toks[:, c0:c0 + n], in_=grp[:, 4 * c0:4 * (c0 + n)])
+
+        def quant_w(h):
+            nc.vector.quantize_mx(out=wc[:, h * 512:(h + 1) * 512].bitcast(FP8X4), scales=ws[:, h * 512:(h + 1) * 512], in_=gw[:, h * 2048:(h + 1) * 2048])
+
+        def make_posb(g):
+            for h in range(2):
+                cols = slice(h * 512, (h + 1) * 512)
+                nc.gpsimd.tensor_tensor(out=posb[g][:, cols], in0=pos_sb[g][:, cols], in1=bbc[:, cols], op=ADD)
+
+        def emit(t, g, dram):
+            o = keep.tile([P, 1024], F32, name="o%d" % t)
+            for h in range(2):
+                cols = slice(h * 512, (h + 1) * 512)
+                acc = psum.tile([P, 512], F32, tag="bank")
+                nc.tensor.matmul_mx(
+                    out=acc[:],
+                    lhsT=tokc[:, t * P:(t + 1) * P].bitcast(FP8X4), lhsT_scale=toks[:, t * P:(t + 1) * P],
+                    rhs=wc[:, cols].bitcast(FP8X4), rhs_scale=ws[:, cols],
+                    start=True, stop=True,
+                )
+                nc.vector.tensor_tensor(out=o[:, cols], in0=acc[:], in1=posb[g][:, cols], op=ADD)
+            nc.sync.dma_start(out=dram, in_=o[:])
+
+        ov = out.rearrange("b (s r) e -> b s r e", r=18)
+        regroup(0, 0, 6)
+        regroup(1, 0, 2)
+        tok_group(0)
+        w_half(0)
+        quant_tok(0, 512)
+        quant_w(0)
+        make_posb(0)
+        w_half(1)
+        quant_w(1)
+        regroup(1, 2, 6)
+        regroup(2, 0, 6)
+        for bi in range(4):
+            emit(bi, 0, ov[bi, :, 0:8, :])
+        tok_group(1)
+        quant_tok(512, 512)
+        make_posb(1)
+        tok_bank(16, 2, perm1, grpw[:, 2048:2304].rearrange("p (x r t) -> p x r t", r=2, t=2))
+        quant_tok(1024, 128)
+        make_posb(2)
+        for bi in range(4):
+            emit(4 + bi, 1, ov[bi, :, 8:16, :])
+        emit(8, 2, out.rearrange("b (s r) e -> (b s) r e", r=18)[:, 16:18, :])

@@ -11,48 +11,56 @@ FP8X4 = mybir.dt.float8_e4m3fn_x4
 ADD = mybir.AluOpType.add
 P = 128
 FLOPS = 2 * 1152 * 512 * 1024
+PIN = True
 
 
 def tile_tubeletembedding_kernel(tc, video, W, b, pos_embed, out):
     nc = tc.nc
     with ExitStack() as ctx:
         keep = ctx.enter_context(tc.tile_pool(name="keep", bufs=1))
-        psum = ctx.enter_context(tc.psum_pool(name="psum", bufs=8))
+        psb = ctx.enter_context(tc.psum_pool(name="psb", bufs=1))
+        psum = ctx.enter_context(tc.psum_pool(name="psum", bufs=6))
+        if PIN:
+            ctx.enter_context(tc.manual_schedule())
+
+        vid = video.rearrange("b t o (h c y) x -> (b t o h) c (y x)", h=2, c=3, y=16)
+        wv = W.rearrange("(a p) k -> p a k", p=P)
+        pv = pos_embed.rearrange("o (s r) e -> (o s) r e", r=18)
+        ov = out.rearrange("b (s r) e -> b s r e", r=18)
+        on = out.rearrange("b (s r) e -> (b s) r e", r=18)
 
         ident = keep.tile([P, P], F32)
         make_identity(nc, ident[:])
+        z = keep.tile([P, 1024], BF16)
+        nc.vector.memset(z[:], 0.0)
+
+        v_sb = keep.tile([P, 3, 1536], BF16)
+        w_sb = keep.tile([P, 8, 512], BF16)
+        pos_sb = [keep.tile([P, 1024], BF16, name="pos%d" % g) for g in range(2)]
+        nc.sync.dma_start(out=w_sb[:, 0:4, :], in_=wv[:, 0:4, :])
+        nc.sync.dma_start(out=z[32:33, :], in_=b.unsqueeze(0))
+        nc.sync.dma_start(out=z[0:32, :], in_=pv[:, 0:2, :])
+        nc.sync.dma_start(out=v_sb[:, 0, :], in_=vid[:, 0, :])
+        nc.sync.dma_start(out=v_sb[:, 1, :], in_=vid[:, 1, :])
+        nc.sync.dma_start(out=pos_sb[0][:], in_=pv[:, 2:10, :])
+        nc.sync.dma_start(out=w_sb[:, 4:8, :], in_=wv[:, 4:8, :])
+        nc.sync.dma_start(out=v_sb[:, 2, :], in_=vid[:, 2, :])
+        nc.sync.dma_start(out=pos_sb[1][:], in_=pv[:, 10:18, :])
+
         perm1 = keep.tile([P, P], F32)
         nc.vector.tensor_copy(
             out=perm1[:].rearrange("p (a h t) -> p a h t", h=2, t=2),
             in_=ident[:].rearrange("p (a t h) -> p a h t", t=2, h=2),
         )
-        ones = keep.tile([P, P], BF16)
-        nc.vector.memset(ones[:], 1.0)
-        bz = keep.tile([P, 1024], BF16)
-        nc.vector.memset(bz[:], 0.0)
-
-        vid = video.rearrange("b t o (h c y) x -> (b t o h) c (y x)", h=2, c=3, y=16)
-        wv = W.rearrange("(a p) k -> p a k", p=P)
-        pv = pos_embed.rearrange("o (s r) e -> (o s) r e", r=18)
-        v_sb = keep.tile([P, 3, 1536], BF16)
-        w_sb = keep.tile([P, 8, 512], BF16)
-        pos_sb = [keep.tile([P, 1024], BF16, name="pos%d" % g) for g in range(3)]
-        nc.sync.dma_start(out=bz[0:1, :], in_=b.unsqueeze(0))
-        nc.sync.dma_start(out=v_sb[:, 0, :], in_=vid[:, 0, :])
-        nc.sync.dma_start(out=v_sb[:, 1, :], in_=vid[:, 1, :])
-        nc.sync.dma_start(out=w_sb[:, 0:4, :], in_=wv[:, 0:4, :])
-        nc.sync.dma_start(out=pos_sb[0][:], in_=pv[:, 0:8, :])
-        nc.sync.dma_start(out=w_sb[:, 4:8, :], in_=wv[:, 4:8, :])
-        nc.sync.dma_start(out=v_sb[:, 2, :], in_=vid[:, 2, :])
-        nc.sync.dma_start(out=pos_sb[1][:], in_=pv[:, 8:16, :])
-        for bi in range(4):
-            nc.sync.dma_start(out=pos_sb[2][32 * bi:32 * (bi + 1), :], in_=pv[:, 16:18, :])
-
-        bbc = keep.tile([P, 1024], F32)
-        for h in range(2):
-            pb = psum.tile([P, 512], F32, tag="bank")
-            nc.tensor.matmul(out=pb[:], lhsT=ones[:], rhs=bz[:, h * 512:(h + 1) * 512], start=True, stop=True)
-            nc.scalar.copy(out=bbc[:, h * 512:(h + 1) * 512], in_=pb[:])
+        sel_n = keep.tile([P, P], BF16)
+        nc.vector.tensor_tensor(
+            out=sel_n[:].rearrange("p (c q) -> p c q", c=4),
+            in0=ident[:, 0:32].unsqueeze(1).to_broadcast([P, 4, 32]),
+            in1=ident[:, 32:33].unsqueeze(1).to_broadcast([P, 4, 32]),
+            op=ADD,
+        )
+        sel_b = keep.tile([P, P], BF16)
+        nc.vector.tensor_copy(out=sel_b[:], in_=ident[:, 32:33].to_broadcast([P, P]))
 
         v2 = keep.tile([P, 4608], BF16)
         v2w = v2[:].bitcast(F32)
@@ -66,6 +74,21 @@ def tile_tubeletembedding_kernel(tc, video, W, b, pos_embed, out):
         ws = keep.tile([P, 1024], U8, align_bytes=64)
         w_w = w_sb[:].rearrange("p a k -> p (a k)").bitcast(F32)
         posb = [keep.tile([P, 1024], F32, name="posb%d" % g) for g in range(3)]
+        o_sb = [keep.tile([P, 1024], F32, name="o%d" % t) for t in range(9)]
+        bbc = [psb.tile([P, 512], F32, name="bbc%d" % h) for h in range(2)]
+        accs = {}
+
+        def half(h):
+            return slice(h * 512, (h + 1) * 512)
+
+        def bias_mm(h):
+            nc.tensor.matmul(out=bbc[h][:], lhsT=sel_b[:], rhs=z[:, half(h)], start=True, stop=True)
+            pn = psum.tile([P, 512], F32, tag="bank", name="pn%d" % h)
+            nc.tensor.matmul(out=pn[:], lhsT=sel_n[:], rhs=z[:, half(h)], start=True, stop=True)
+            nc.scalar.copy(out=posb[2][:, half(h)], in_=pn[:])
+
+        def make_posb(g, h):
+            nc.vector.tensor_tensor(out=posb[g][:, half(h)], in0=bbc[h][:], in1=pos_sb[g][:, half(h)], op=ADD)
 
         def regroup(c, j0, j1):
             nc.vector.tensor_copy(
@@ -73,75 +96,123 @@ def tile_tubeletembedding_kernel(tc, video, W, b, pos_embed, out):
                 in_=v_sb[:, c, :].rearrange("p (y j x) -> p j y x", j=6, x=16)[:, j0:j1, :, :],
             )
 
-        def tok_bank(r0, n, perm, dst):
-            pt = psum.tile([P, 512], F32, tag="bank")
+        def tok_bank(r0, n, dst):
+            pt = psum.tile([P, 512], F32, tag="bank", name="pt%d" % r0)
             for i in range(n):
                 r = r0 + i
-                nc.tensor.transpose(pt[:, i * P:(i + 1) * P], v2w[:, r * P:(r + 1) * P], perm[:])
+                nc.tensor.transpose(pt[:, i * P:(i + 1) * P], v2w[:, r * P:(r + 1) * P], perm1[:])
             nc.scalar.copy(out=dst, in_=pt[:, 0:n * P].rearrange("p (r x t) -> p x r t", r=n, t=2))
 
-        def tok_group(g):
-            view = grpw[:, g * 1024:(g + 1) * 1024].rearrange("p (x r t) -> p x r t", r=8, t=2)
-            for q in range(2):
-                tok_bank(8 * g + 4 * q, 4, perm1, view[:, :, 4 * q:4 * q + 4, :])
+        def tok_group_bank(g, q):
+            view = grpw[:, 256 + g * 1024:256 + (g + 1) * 1024].rearrange("p (x r t) -> p x r t", r=8, t=2)
+            tok_bank(2 + 8 * g + 4 * q, 4, view[:, :, 4 * q:4 * q + 4, :])
 
-        def w_half(h):
-            for q in range(2):
-                a0 = 4 * h + 2 * q
-                pt = psum.tile([P, 512], F32, tag="bank")
-                for i in range(4):
-                    a, u = a0 + i // 2, i % 2
-                    nc.tensor.transpose(pt[:, i * P:(i + 1) * P], w_w[:, a * 256 + u * P:a * 256 + (u + 1) * P], ident[:])
-                nc.vector.tensor_copy(
-                    out=gww[:, a0 * 256:(a0 + 2) * 256].rearrange("p (a e u) -> p a e u", a=2, u=2),
-                    in_=pt[:].rearrange("p (a u e) -> p a e u", a=2, u=2),
-                )
+        def w_bank(h, q):
+            a0 = 4 * h + 2 * q
+            pt = psum.tile([P, 512], F32, tag="bank", name="pw%d" % a0)
+            for i in range(4):
+                a, u = a0 + i // 2, i % 2
+                nc.tensor.transpose(pt[:, i * P:(i + 1) * P], w_w[:, a * 256 + u * P:a * 256 + (u + 1) * P], ident[:])
+            nc.scalar.copy(
+                out=gww[:, a0 * 256:(a0 + 2) * 256].rearrange("p (a e u) -> p a e u", a=2, u=2),
+                in_=pt[:].rearrange("p (a u e) -> p a e u", a=2, u=2),
+            )
 
         def quant_tok(c0, n):
             nc.vector.quantize_mx(out=tokc[:, c0:c0 + n].bitcast(FP8X4), scales=toks[:, c0:c0 + n], in_=grp[:, 4 * c0:4 * (c0 + n)])
 
         def quant_w(h):
-            nc.vector.quantize_mx(out=wc[:, h * 512:(h + 1) * 512].bitcast(FP8X4), scales=ws[:, h * 512:(h + 1) * 512], in_=gw[:, h * 2048:(h + 1) * 2048])
+            nc.vector.quantize_mx(out=wc[:, half(h)].bitcast(FP8X4), scales=ws[:, half(h)], in_=gw[:, h * 2048:(h + 1) * 2048])
 
-        def make_posb(g):
-            for h in range(2):
-                cols = slice(h * 512, (h + 1) * 512)
-                nc.gpsimd.tensor_tensor(out=posb[g][:, cols], in0=pos_sb[g][:, cols], in1=bbc[:, cols], op=ADD)
+        def mx(t, h):
+            acc = psum.tile([P, 512], F32, tag="bank", name="acc%d_%d" % (t, h))
+            nc.tensor.matmul_mx(
+                out=acc[:],
+                lhsT=tokc[:, t * P:(t + 1) * P].bitcast(FP8X4), lhsT_scale=toks[:, t * P:(t + 1) * P],
+                rhs=wc[:, half(h)].bitcast(FP8X4), rhs_scale=ws[:, half(h)],
+                start=True, stop=True,
+            )
+            accs[(t, h)] = acc
 
-        def emit(t, g, dram):
-            o = keep.tile([P, 1024], F32, name="o%d" % t)
-            for h in range(2):
-                cols = slice(h * 512, (h + 1) * 512)
-                acc = psum.tile([P, 512], F32, tag="bank")
-                nc.tensor.matmul_mx(
-                    out=acc[:],
-                    lhsT=tokc[:, t * P:(t + 1) * P].bitcast(FP8X4), lhsT_scale=toks[:, t * P:(t + 1) * P],
-                    rhs=wc[:, cols].bitcast(FP8X4), rhs_scale=ws[:, cols],
-                    start=True, stop=True,
-                )
-                nc.vector.tensor_tensor(out=o[:, cols], in0=acc[:], in1=posb[g][:, cols], op=ADD)
-            nc.sync.dma_start(out=dram, in_=o[:])
+        def group_of(t):
+            return 2 if t == 0 else (t - 1) // 4
 
-        ov = out.rearrange("b (s r) e -> b s r e", r=18)
-        regroup(0, 0, 6)
-        regroup(1, 0, 2)
-        tok_group(0)
-        w_half(0)
-        quant_tok(0, 512)
+        def add_v(t, h):
+            nc.vector.tensor_tensor(out=o_sb[t][:, half(h)], in0=accs[(t, h)][:], in1=posb[group_of(t)][:, half(h)], op=ADD)
+
+        def add_sg(t, h):
+            tmp = keep.tile([P, 512], F32, name="tmp%d_%d" % (t, h))
+            nc.scalar.copy(out=tmp[:], in_=accs[(t, h)][:])
+            nc.gpsimd.tensor_tensor(out=o_sb[t][:, half(h)], in0=tmp[:], in1=posb[group_of(t)][:, half(h)], op=ADD)
+
+        def dram(t, cols):
+            if t == 0:
+                return on[:, 0:2, cols]
+            g, bi = (t - 1) // 4, (t - 1) % 4
+            return ov[bi, :, 2 + 8 * g:10 + 8 * g, cols]
+
+        def store(t, h=None):
+            cols = slice(0, 1024) if h is None else half(h)
+            nc.sync.dma_start(out=dram(t, cols), in_=o_sb[t][:, cols])
+
+        w_bank(0, 0)
+        w_bank(0, 1)
+        bias_mm(0)
+        regroup(0, 0, 2)
+        regroup(0, 2, 6)
+        tok_bank(0, 2, grpw[:, 0:256].rearrange("p (x r t) -> p x r t", r=2, t=2))
+        tok_group_bank(0, 0)
+        regroup(1, 0, 4)
         quant_w(0)
-        make_posb(0)
-        w_half(1)
-        quant_w(1)
-        regroup(1, 2, 6)
+        tok_group_bank(0, 1)
+        quant_tok(0, 128)
+        make_posb(0, 0)
+        mx(0, 0)
+        bias_mm(1)
+        w_bank(1, 0)
+        w_bank(1, 1)
+        add_v(0, 0)
+        store(0, 0)
+        quant_tok(128, 512)
+        regroup(1, 4, 6)
         regroup(2, 0, 6)
-        for bi in range(4):
-            emit(bi, 0, ov[bi, :, 0:8, :])
-        tok_group(1)
-        quant_tok(512, 512)
-        make_posb(1)
-        tok_bank(16, 2, perm1, grpw[:, 2048:2304].rearrange("p (x r t) -> p x r t", r=2, t=2))
-        quant_tok(1024, 128)
-        make_posb(2)
-        for bi in range(4):
-            emit(4 + bi, 1, ov[bi, :, 8:16, :])
-        emit(8, 2, out.rearrange("b (s r) e -> (b s) r e", r=18)[:, 16:18, :])
+        for t in (1, 2, 3, 4):
+            mx(t, 0)
+        tok_group_bank(1, 0)
+        tok_group_bank(1, 1)
+        add_v(1, 0)
+        store(1, 0)
+        add_v(2, 0)
+        store(2, 0)
+        quant_w(1)
+        make_posb(0, 1)
+        add_v(3, 0)
+        mx(3, 1)
+        add_sg(3, 1)
+        mx(0, 1)
+        add_v(4, 0)
+        mx(4, 1)
+        add_sg(4, 1)
+        add_v(0, 1)
+        store(0, 1)
+        mx(1, 1)
+        mx(2, 1)
+        quant_tok(640, 512)
+        add_v(1, 1)
+        store(1, 1)
+        add_v(2, 1)
+        store(2, 1)
+        store(3)
+        store(4)
+        make_posb(1, 0)
+        make_posb(1, 1)
+        for t in (5, 6, 7):
+            mx(t, 1)
+            add_sg(t, 1)
+            mx(t, 0)
+            add_v(t, 0)
+            store(t)
+        for h in range(2):
+            mx(8, h)
+            add_v(8, h)
+            store(8, h)

@@ -11,17 +11,14 @@ FP8X4 = mybir.dt.float8_e4m3fn_x4
 ADD = mybir.AluOpType.add
 P = 128
 FLOPS = 2 * 1152 * 512 * 1024
-PIN = True
 
 
 def tile_tubeletembedding_kernel(tc, video, W, b, pos_embed, out):
     nc = tc.nc
     with ExitStack() as ctx:
         keep = ctx.enter_context(tc.tile_pool(name="keep", bufs=1))
-        psb = ctx.enter_context(tc.psum_pool(name="psb", bufs=1))
-        psum = ctx.enter_context(tc.psum_pool(name="psum", bufs=6))
-        if PIN:
-            ctx.enter_context(tc.manual_schedule())
+        psum = ctx.enter_context(tc.psum_pool(name="psum", bufs=8))
+        ctx.enter_context(tc.manual_schedule())
 
         vid = video.rearrange("b t o (h c y) x -> (b t o h) c (y x)", h=2, c=3, y=16)
         wv = W.rearrange("(a p) k -> p a k", p=P)
@@ -37,14 +34,14 @@ def tile_tubeletembedding_kernel(tc, video, W, b, pos_embed, out):
         v_sb = keep.tile([P, 3, 1536], BF16)
         w_sb = keep.tile([P, 8, 512], BF16)
         pos_sb = [keep.tile([P, 1024], BF16, name="pos%d" % g) for g in range(2)]
-        nc.sync.dma_start(out=w_sb[:, 0:4, :], in_=wv[:, 0:4, :])
+        nc.sync.dma_start(out=v_sb[:, 2, :], in_=vid[:, 2, :])
         nc.sync.dma_start(out=z[32:33, :], in_=b.unsqueeze(0))
         nc.sync.dma_start(out=z[0:32, :], in_=pv[:, 0:2, :])
         nc.sync.dma_start(out=v_sb[:, 0, :], in_=vid[:, 0, :])
         nc.sync.dma_start(out=v_sb[:, 1, :], in_=vid[:, 1, :])
-        nc.sync.dma_start(out=pos_sb[0][:], in_=pv[:, 2:10, :])
+        nc.sync.dma_start(out=w_sb[:, 0:4, :], in_=wv[:, 0:4, :])
         nc.sync.dma_start(out=w_sb[:, 4:8, :], in_=wv[:, 4:8, :])
-        nc.sync.dma_start(out=v_sb[:, 2, :], in_=vid[:, 2, :])
+        nc.sync.dma_start(out=pos_sb[0][:], in_=pv[:, 2:10, :])
         nc.sync.dma_start(out=pos_sb[1][:], in_=pv[:, 10:18, :])
 
         perm1 = keep.tile([P, P], F32)
@@ -75,20 +72,36 @@ def tile_tubeletembedding_kernel(tc, video, W, b, pos_embed, out):
         w_w = w_sb[:].rearrange("p a k -> p (a k)").bitcast(F32)
         posb = [keep.tile([P, 1024], F32, name="posb%d" % g) for g in range(3)]
         o_sb = [keep.tile([P, 1024], F32, name="o%d" % t) for t in range(9)]
-        bbc = [psb.tile([P, 512], F32, name="bbc%d" % h) for h in range(2)]
+        bbcs = keep.tile([P, 1024], F32)
+        bbc = {}
         accs = {}
 
         def half(h):
             return slice(h * 512, (h + 1) * 512)
 
-        def bias_mm(h):
+        def copy_out(eng, dst, src):
+            if eng == "V":
+                nc.vector.tensor_copy(out=dst, in_=src)
+            else:
+                nc.scalar.copy(out=dst, in_=src)
+
+        def bbc_mm(h):
+            bbc[h] = psum.tile([P, 512], F32, tag="bank", name="bbc%d" % h)
             nc.tensor.matmul(out=bbc[h][:], lhsT=sel_b[:], rhs=z[:, half(h)], start=True, stop=True)
+
+        def pn_mm(h):
             pn = psum.tile([P, 512], F32, tag="bank", name="pn%d" % h)
             nc.tensor.matmul(out=pn[:], lhsT=sel_n[:], rhs=z[:, half(h)], start=True, stop=True)
             nc.scalar.copy(out=posb[2][:, half(h)], in_=pn[:])
 
-        def make_posb(g, h):
-            nc.vector.tensor_tensor(out=posb[g][:, half(h)], in0=bbc[h][:], in1=pos_sb[g][:, half(h)], op=ADD)
+        def bbc_copy(h):
+            nc.scalar.copy(out=bbcs[:, half(h)], in_=bbc[h][:])
+
+        def make_posb(g, h, eng="V"):
+            if eng == "V":
+                nc.vector.tensor_tensor(out=posb[g][:, half(h)], in0=bbc[h][:], in1=pos_sb[g][:, half(h)], op=ADD)
+            else:
+                nc.gpsimd.tensor_tensor(out=posb[g][:, half(h)], in0=pos_sb[g][:, half(h)], in1=bbcs[:, half(h)], op=ADD)
 
         def regroup(c, j0, j1):
             nc.vector.tensor_copy(
@@ -96,26 +109,30 @@ def tile_tubeletembedding_kernel(tc, video, W, b, pos_embed, out):
                 in_=v_sb[:, c, :].rearrange("p (y j x) -> p j y x", j=6, x=16)[:, j0:j1, :, :],
             )
 
-        def tok_bank(r0, n, dst):
+        def tok_t(r0, n, dst, eng):
             pt = psum.tile([P, 512], F32, tag="bank", name="pt%d" % r0)
             for i in range(n):
                 r = r0 + i
                 nc.tensor.transpose(pt[:, i * P:(i + 1) * P], v2w[:, r * P:(r + 1) * P], perm1[:])
-            nc.scalar.copy(out=dst, in_=pt[:, 0:n * P].rearrange("p (r x t) -> p x r t", r=n, t=2))
+            copy_out(eng, dst, pt[:, 0:n * P].rearrange("p (r x t) -> p x r t", r=n, t=2))
 
-        def tok_group_bank(g, q):
+        def tok_bank(r0, n, eng="S"):
+            tok_t(r0, n, grpw[:, 0:256].rearrange("p (x r t) -> p x r t", r=2, t=2), eng)
+
+        def tok_group_bank(g, q, eng="S"):
             view = grpw[:, 256 + g * 1024:256 + (g + 1) * 1024].rearrange("p (x r t) -> p x r t", r=8, t=2)
-            tok_bank(2 + 8 * g + 4 * q, 4, view[:, :, 4 * q:4 * q + 4, :])
+            tok_t(2 + 8 * g + 4 * q, 4, view[:, :, 4 * q:4 * q + 4, :], eng)
 
-        def w_bank(h, q):
+        def w_bank(h, q, eng="S"):
             a0 = 4 * h + 2 * q
             pt = psum.tile([P, 512], F32, tag="bank", name="pw%d" % a0)
             for i in range(4):
                 a, u = a0 + i // 2, i % 2
                 nc.tensor.transpose(pt[:, i * P:(i + 1) * P], w_w[:, a * 256 + u * P:a * 256 + (u + 1) * P], ident[:])
-            nc.scalar.copy(
-                out=gww[:, a0 * 256:(a0 + 2) * 256].rearrange("p (a e u) -> p a e u", a=2, u=2),
-                in_=pt[:].rearrange("p (a u e) -> p a e u", a=2, u=2),
+            copy_out(
+                eng,
+                gww[:, a0 * 256:(a0 + 2) * 256].rearrange("p (a e u) -> p a e u", a=2, u=2),
+                pt[:].rearrange("p (a u e) -> p a e u", a=2, u=2),
             )
 
         def quant_tok(c0, n):
@@ -155,64 +172,81 @@ def tile_tubeletembedding_kernel(tc, video, W, b, pos_embed, out):
             cols = slice(0, 1024) if h is None else half(h)
             nc.sync.dma_start(out=dram(t, cols), in_=o_sb[t][:, cols])
 
-        w_bank(0, 0)
-        w_bank(0, 1)
-        bias_mm(0)
-        regroup(0, 0, 2)
-        regroup(0, 2, 6)
-        tok_bank(0, 2, grpw[:, 0:256].rearrange("p (x r t) -> p x r t", r=2, t=2))
-        tok_group_bank(0, 0)
-        regroup(1, 0, 4)
-        quant_w(0)
-        tok_group_bank(0, 1)
-        quant_tok(0, 128)
-        make_posb(0, 0)
-        mx(0, 0)
-        bias_mm(1)
-        w_bank(1, 0)
-        w_bank(1, 1)
-        add_v(0, 0)
-        store(0, 0)
-        quant_tok(128, 512)
-        regroup(1, 4, 6)
+        bbc_mm(1)
+        bbc_mm(0)
         regroup(2, 0, 6)
-        for t in (1, 2, 3, 4):
-            mx(t, 0)
-        tok_group_bank(1, 0)
+        bbc_copy(0)
+        regroup(0, 0, 2)
         tok_group_bank(1, 1)
-        add_v(1, 0)
-        store(1, 0)
-        add_v(2, 0)
-        store(2, 0)
+        regroup(0, 2, 6)
+        regroup(1, 4, 6)
+        tok_bank(0, 2)
+        regroup(1, 0, 4)
+        tok_group_bank(0, 0, "V")
+        tok_group_bank(1, 0, "V")
+        quant_tok(640, 512)
+        w_bank(0, 1)
+        quant_tok(0, 128)
+        w_bank(0, 0)
+        tok_group_bank(0, 1)
+        w_bank(1, 1)
+        quant_w(0)
+        make_posb(0, 0)
+        w_bank(1, 0)
+        mx(8, 0)
+        make_posb(1, 0, "G")
+        mx(5, 0)
+        make_posb(1, 1)
+        mx(6, 0)
+        mx(7, 0)
         quant_w(1)
-        make_posb(0, 1)
-        add_v(3, 0)
+        quant_tok(128, 512)
+        add_v(5, 0)
+        mx(7, 1)
+        add_sg(8, 0)
+        add_v(6, 0)
+        mx(6, 1)
+        add_sg(7, 1)
+        store(5, 0)
+        bbc_copy(1)
+        mx(4, 0)
+        add_v(7, 0)
+        mx(1, 0)
+        mx(1, 1)
+        make_posb(0, 1, "G")
+        mx(8, 1)
+        mx(5, 1)
+        store(8, 0)
+        add_v(6, 1)
+        store(6, 0)
         mx(3, 1)
-        add_sg(3, 1)
-        mx(0, 1)
-        add_v(4, 0)
+        mx(2, 0)
+        mx(2, 1)
+        add_v(1, 0)
+        add_sg(4, 0)
+        add_v(8, 1)
+        add_sg(5, 1)
+        store(7)
+        add_v(1, 1)
         mx(4, 1)
         add_sg(4, 1)
-        add_v(0, 1)
-        store(0, 1)
-        mx(1, 1)
-        mx(2, 1)
-        quant_tok(640, 512)
-        add_v(1, 1)
-        store(1, 1)
+        store(6, 1)
+        store(8, 1)
+        store(4, 0)
+        mx(3, 0)
+        store(1)
+        add_v(2, 0)
         add_v(2, 1)
-        store(2, 1)
+        pn_mm(1)
+        pn_mm(0)
+        add_v(3, 0)
+        add_v(3, 1)
+        mx(0, 1)
+        mx(0, 0)
+        add_v(0, 1)
+        store(5, 1)
+        add_v(0, 0)
+        store(2)
+        store(4, 1)
         store(3)
-        store(4)
-        make_posb(1, 0)
-        make_posb(1, 1)
-        for t in (5, 6, 7):
-            mx(t, 1)
-            add_sg(t, 1)
-            mx(t, 0)
-            add_v(t, 0)
-            store(t)
-        for h in range(2):
-            mx(8, h)
-            add_v(8, h)
-            store(8, h)
+        store(0)

@@ -11,14 +11,18 @@ FP8X4 = mybir.dt.float8_e4m3fn_x4
 ADD = mybir.AluOpType.add
 P = 128
 FLOPS = 2 * 1152 * 512 * 1024
+PIN = True
+N_WARM = 3
 
 
 def tile_tubeletembedding_kernel(tc, video, W, b, pos_embed, out):
     nc = tc.nc
     with ExitStack() as ctx:
         keep = ctx.enter_context(tc.tile_pool(name="keep", bufs=1))
-        psum = ctx.enter_context(tc.psum_pool(name="psum", bufs=8))
-        ctx.enter_context(tc.manual_schedule())
+        psb = ctx.enter_context(tc.psum_pool(name="psb", bufs=1))
+        psum = ctx.enter_context(tc.psum_pool(name="psum", bufs=6))
+        if PIN:
+            ctx.enter_context(tc.manual_schedule())
 
         vid = video.rearrange("b t o (h c y) x -> (b t o h) c (y x)", h=2, c=3, y=16)
         wv = W.rearrange("(a p) k -> p a k", p=P)
@@ -30,18 +34,20 @@ def tile_tubeletembedding_kernel(tc, video, W, b, pos_embed, out):
         make_identity(nc, ident[:])
         z = keep.tile([P, 1024], BF16)
         nc.vector.memset(z[:], 0.0)
+        dzb = keep.tile([P, 512], BF16)
+        nc.vector.memset(dzb[:], 0.0)
 
         v_sb = keep.tile([P, 3, 1536], BF16)
         w_sb = keep.tile([P, 8, 512], BF16)
         pos_sb = [keep.tile([P, 1024], BF16, name="pos%d" % g) for g in range(2)]
-        nc.sync.dma_start(out=v_sb[:, 2, :], in_=vid[:, 2, :])
+        nc.sync.dma_start(out=w_sb[:, 0:4, :], in_=wv[:, 0:4, :])
         nc.sync.dma_start(out=z[32:33, :], in_=b.unsqueeze(0))
         nc.sync.dma_start(out=z[0:32, :], in_=pv[:, 0:2, :])
         nc.sync.dma_start(out=v_sb[:, 0, :], in_=vid[:, 0, :])
         nc.sync.dma_start(out=v_sb[:, 1, :], in_=vid[:, 1, :])
-        nc.sync.dma_start(out=w_sb[:, 0:4, :], in_=wv[:, 0:4, :])
-        nc.sync.dma_start(out=w_sb[:, 4:8, :], in_=wv[:, 4:8, :])
         nc.sync.dma_start(out=pos_sb[0][:], in_=pv[:, 2:10, :])
+        nc.sync.dma_start(out=w_sb[:, 4:8, :], in_=wv[:, 4:8, :])
+        nc.sync.dma_start(out=v_sb[:, 2, :], in_=vid[:, 2, :])
         nc.sync.dma_start(out=pos_sb[1][:], in_=pv[:, 10:18, :])
 
         perm1 = keep.tile([P, P], F32)
@@ -58,6 +64,9 @@ def tile_tubeletembedding_kernel(tc, video, W, b, pos_embed, out):
         )
         sel_b = keep.tile([P, P], BF16)
         nc.vector.tensor_copy(out=sel_b[:], in_=ident[:, 32:33].to_broadcast([P, P]))
+        pd = psum.tile([P, 512], F32, tag="bank", name="pd")
+        for i in range(N_WARM):
+            nc.tensor.matmul(out=pd[:], lhsT=sel_b[:], rhs=dzb[:], start=True, stop=True)
 
         v2 = keep.tile([P, 4608], BF16)
         v2w = v2[:].bitcast(F32)
@@ -72,36 +81,20 @@ def tile_tubeletembedding_kernel(tc, video, W, b, pos_embed, out):
         w_w = w_sb[:].rearrange("p a k -> p (a k)").bitcast(F32)
         posb = [keep.tile([P, 1024], F32, name="posb%d" % g) for g in range(3)]
         o_sb = [keep.tile([P, 1024], F32, name="o%d" % t) for t in range(9)]
-        bbcs = keep.tile([P, 1024], F32)
-        bbc = {}
+        bbc = [psb.tile([P, 512], F32, name="bbc%d" % h) for h in range(2)]
         accs = {}
 
         def half(h):
             return slice(h * 512, (h + 1) * 512)
 
-        def copy_out(eng, dst, src):
-            if eng == "V":
-                nc.vector.tensor_copy(out=dst, in_=src)
-            else:
-                nc.scalar.copy(out=dst, in_=src)
-
-        def bbc_mm(h):
-            bbc[h] = psum.tile([P, 512], F32, tag="bank", name="bbc%d" % h)
+        def bias_mm(h):
             nc.tensor.matmul(out=bbc[h][:], lhsT=sel_b[:], rhs=z[:, half(h)], start=True, stop=True)
-
-        def pn_mm(h):
             pn = psum.tile([P, 512], F32, tag="bank", name="pn%d" % h)
             nc.tensor.matmul(out=pn[:], lhsT=sel_n[:], rhs=z[:, half(h)], start=True, stop=True)
             nc.scalar.copy(out=posb[2][:, half(h)], in_=pn[:])
 
-        def bbc_copy(h):
-            nc.scalar.copy(out=bbcs[:, half(h)], in_=bbc[h][:])
-
-        def make_posb(g, h, eng="V"):
-            if eng == "V":
-                nc.vector.tensor_tensor(out=posb[g][:, half(h)], in0=bbc[h][:], in1=pos_sb[g][:, half(h)], op=ADD)
-            else:
-                nc.gpsimd.tensor_tensor(out=posb[g][:, half(h)], in0=pos_sb[g][:, half(h)], in1=bbcs[:, half(h)], op=ADD)
+        def make_posb(g, h):
+            nc.vector.tensor_tensor(out=posb[g][:, half(h)], in0=bbc[h][:], in1=pos_sb[g][:, half(h)], op=ADD)
 
         def regroup(c, j0, j1):
             nc.vector.tensor_copy(
@@ -109,30 +102,26 @@ def tile_tubeletembedding_kernel(tc, video, W, b, pos_embed, out):
                 in_=v_sb[:, c, :].rearrange("p (y j x) -> p j y x", j=6, x=16)[:, j0:j1, :, :],
             )
 
-        def tok_t(r0, n, dst, eng):
+        def tok_bank(r0, n, dst):
             pt = psum.tile([P, 512], F32, tag="bank", name="pt%d" % r0)
             for i in range(n):
                 r = r0 + i
                 nc.tensor.transpose(pt[:, i * P:(i + 1) * P], v2w[:, r * P:(r + 1) * P], perm1[:])
-            copy_out(eng, dst, pt[:, 0:n * P].rearrange("p (r x t) -> p x r t", r=n, t=2))
+            nc.scalar.copy(out=dst, in_=pt[:, 0:n * P].rearrange("p (r x t) -> p x r t", r=n, t=2))
 
-        def tok_bank(r0, n, eng="S"):
-            tok_t(r0, n, grpw[:, 0:256].rearrange("p (x r t) -> p x r t", r=2, t=2), eng)
-
-        def tok_group_bank(g, q, eng="S"):
+        def tok_group_bank(g, q):
             view = grpw[:, 256 + g * 1024:256 + (g + 1) * 1024].rearrange("p (x r t) -> p x r t", r=8, t=2)
-            tok_t(2 + 8 * g + 4 * q, 4, view[:, :, 4 * q:4 * q + 4, :], eng)
+            tok_bank(2 + 8 * g + 4 * q, 4, view[:, :, 4 * q:4 * q + 4, :])
 
-        def w_bank(h, q, eng="S"):
+        def w_bank(h, q):
             a0 = 4 * h + 2 * q
             pt = psum.tile([P, 512], F32, tag="bank", name="pw%d" % a0)
             for i in range(4):
                 a, u = a0 + i // 2, i % 2
                 nc.tensor.transpose(pt[:, i * P:(i + 1) * P], w_w[:, a * 256 + u * P:a * 256 + (u + 1) * P], ident[:])
-            copy_out(
-                eng,
-                gww[:, a0 * 256:(a0 + 2) * 256].rearrange("p (a e u) -> p a e u", a=2, u=2),
-                pt[:].rearrange("p (a u e) -> p a e u", a=2, u=2),
+            nc.scalar.copy(
+                out=gww[:, a0 * 256:(a0 + 2) * 256].rearrange("p (a e u) -> p a e u", a=2, u=2),
+                in_=pt[:].rearrange("p (a u e) -> p a e u", a=2, u=2),
             )
 
         def quant_tok(c0, n):
@@ -172,81 +161,64 @@ def tile_tubeletembedding_kernel(tc, video, W, b, pos_embed, out):
             cols = slice(0, 1024) if h is None else half(h)
             nc.sync.dma_start(out=dram(t, cols), in_=o_sb[t][:, cols])
 
-        bbc_mm(1)
-        bbc_mm(0)
-        regroup(2, 0, 6)
-        bbc_copy(0)
-        regroup(0, 0, 2)
-        tok_group_bank(1, 1)
-        regroup(0, 2, 6)
-        regroup(1, 4, 6)
-        tok_bank(0, 2)
-        regroup(1, 0, 4)
-        tok_group_bank(0, 0, "V")
-        tok_group_bank(1, 0, "V")
-        quant_tok(640, 512)
-        w_bank(0, 1)
-        quant_tok(0, 128)
         w_bank(0, 0)
-        tok_group_bank(0, 1)
-        w_bank(1, 1)
+        w_bank(0, 1)
+        bias_mm(0)
+        regroup(0, 0, 2)
+        regroup(0, 2, 6)
+        tok_bank(0, 2, grpw[:, 0:256].rearrange("p (x r t) -> p x r t", r=2, t=2))
+        tok_group_bank(0, 0)
+        regroup(1, 0, 4)
         quant_w(0)
+        tok_group_bank(0, 1)
+        quant_tok(0, 128)
         make_posb(0, 0)
+        mx(0, 0)
+        bias_mm(1)
         w_bank(1, 0)
-        mx(8, 0)
-        make_posb(1, 0, "G")
-        mx(5, 0)
-        make_posb(1, 1)
-        mx(6, 0)
-        mx(7, 0)
-        quant_w(1)
+        w_bank(1, 1)
+        add_v(0, 0)
+        store(0, 0)
         quant_tok(128, 512)
-        add_v(5, 0)
-        mx(7, 1)
-        add_sg(8, 0)
-        add_v(6, 0)
-        mx(6, 1)
-        add_sg(7, 1)
-        store(5, 0)
-        bbc_copy(1)
-        mx(4, 0)
-        add_v(7, 0)
-        mx(1, 0)
-        mx(1, 1)
-        make_posb(0, 1, "G")
-        mx(8, 1)
-        mx(5, 1)
-        store(8, 0)
-        add_v(6, 1)
-        store(6, 0)
-        mx(3, 1)
-        mx(2, 0)
-        mx(2, 1)
+        regroup(1, 4, 6)
+        regroup(2, 0, 6)
+        for t in (1, 2, 3, 4):
+            mx(t, 0)
+        tok_group_bank(1, 0)
+        tok_group_bank(1, 1)
         add_v(1, 0)
-        add_sg(4, 0)
-        add_v(8, 1)
-        add_sg(5, 1)
-        store(7)
-        add_v(1, 1)
+        store(1, 0)
+        add_v(2, 0)
+        store(2, 0)
+        quant_w(1)
+        make_posb(0, 1)
+        add_v(3, 0)
+        mx(3, 1)
+        add_sg(3, 1)
+        mx(0, 1)
+        add_v(4, 0)
         mx(4, 1)
         add_sg(4, 1)
-        store(6, 1)
-        store(8, 1)
-        store(4, 0)
-        mx(3, 0)
-        store(1)
-        add_v(2, 0)
-        add_v(2, 1)
-        pn_mm(1)
-        pn_mm(0)
-        add_v(3, 0)
-        add_v(3, 1)
-        mx(0, 1)
-        mx(0, 0)
         add_v(0, 1)
-        store(5, 1)
-        add_v(0, 0)
-        store(2)
-        store(4, 1)
+        store(0, 1)
+        mx(1, 1)
+        mx(2, 1)
+        quant_tok(640, 512)
+        add_v(1, 1)
+        store(1, 1)
+        add_v(2, 1)
+        store(2, 1)
         store(3)
-        store(0)
+        store(4)
+        make_posb(1, 0)
+        make_posb(1, 1)
+        for t in (5, 6, 7):
+            mx(t, 1)
+            add_sg(t, 1)
+            mx(t, 0)
+            add_v(t, 0)
+            store(t)
+        for h in range(2):
+            mx(8, h)
+            add_v(8, h)
+            store(8, h)

@@ -11,18 +11,14 @@ FP8X4 = mybir.dt.float8_e4m3fn_x4
 ADD = mybir.AluOpType.add
 P = 128
 FLOPS = 2 * 1152 * 512 * 1024
-PIN = True
-N_WARM = 3
 
 
 def tile_tubeletembedding_kernel(tc, video, W, b, pos_embed, out):
     nc = tc.nc
     with ExitStack() as ctx:
         keep = ctx.enter_context(tc.tile_pool(name="keep", bufs=1))
-        psb = ctx.enter_context(tc.psum_pool(name="psb", bufs=1))
-        psum = ctx.enter_context(tc.psum_pool(name="psum", bufs=6))
-        if PIN:
-            ctx.enter_context(tc.manual_schedule())
+        psum = ctx.enter_context(tc.psum_pool(name="psum", bufs=8))
+        ctx.enter_context(tc.manual_schedule())
 
         vid = video.rearrange("b t o (h c y) x -> (b t o h) c (y x)", h=2, c=3, y=16)
         wv = W.rearrange("(a p) k -> p a k", p=P)
@@ -34,21 +30,19 @@ def tile_tubeletembedding_kernel(tc, video, W, b, pos_embed, out):
         make_identity(nc, ident[:])
         z = keep.tile([P, 1024], BF16)
         nc.vector.memset(z[:], 0.0)
-        dzb = keep.tile([P, 512], BF16)
-        nc.vector.memset(dzb[:], 0.0)
 
         v_sb = keep.tile([P, 3, 1536], BF16)
         w_sb = keep.tile([P, 8, 512], BF16)
         pos_sb = [keep.tile([P, 1024], BF16, name="pos%d" % g) for g in range(2)]
+        nc.sync.dma_start(out=v_sb[:, 0, :], in_=vid[:, 0, :])
         nc.sync.dma_start(out=w_sb[:, 0:4, :], in_=wv[:, 0:4, :])
         nc.sync.dma_start(out=z[32:33, :], in_=b.unsqueeze(0))
+        nc.sync.dma_start(out=v_sb[:, 2, :], in_=vid[:, 2, :])
         nc.sync.dma_start(out=z[0:32, :], in_=pv[:, 0:2, :])
-        nc.sync.dma_start(out=v_sb[:, 0, :], in_=vid[:, 0, :])
         nc.sync.dma_start(out=v_sb[:, 1, :], in_=vid[:, 1, :])
+        nc.sync.dma_start(out=pos_sb[1][:], in_=pv[:, 10:18, :])
         nc.sync.dma_start(out=pos_sb[0][:], in_=pv[:, 2:10, :])
         nc.sync.dma_start(out=w_sb[:, 4:8, :], in_=wv[:, 4:8, :])
-        nc.sync.dma_start(out=v_sb[:, 2, :], in_=vid[:, 2, :])
-        nc.sync.dma_start(out=pos_sb[1][:], in_=pv[:, 10:18, :])
 
         perm1 = keep.tile([P, P], F32)
         nc.vector.tensor_copy(
@@ -64,9 +58,6 @@ def tile_tubeletembedding_kernel(tc, video, W, b, pos_embed, out):
         )
         sel_b = keep.tile([P, P], BF16)
         nc.vector.tensor_copy(out=sel_b[:], in_=ident[:, 32:33].to_broadcast([P, P]))
-        pd = psum.tile([P, 512], F32, tag="bank", name="pd")
-        for i in range(N_WARM):
-            nc.tensor.matmul(out=pd[:], lhsT=sel_b[:], rhs=dzb[:], start=True, stop=True)
 
         v2 = keep.tile([P, 4608], BF16)
         v2w = v2[:].bitcast(F32)
@@ -81,20 +72,36 @@ def tile_tubeletembedding_kernel(tc, video, W, b, pos_embed, out):
         w_w = w_sb[:].rearrange("p a k -> p (a k)").bitcast(F32)
         posb = [keep.tile([P, 1024], F32, name="posb%d" % g) for g in range(3)]
         o_sb = [keep.tile([P, 1024], F32, name="o%d" % t) for t in range(9)]
-        bbc = [psb.tile([P, 512], F32, name="bbc%d" % h) for h in range(2)]
+        bbcs = keep.tile([P, 1024], F32)
+        bbc = {}
         accs = {}
 
         def half(h):
             return slice(h * 512, (h + 1) * 512)
 
-        def bias_mm(h):
+        def copy_out(eng, dst, src):
+            if eng == "V":
+                nc.vector.tensor_copy(out=dst, in_=src)
+            else:
+                nc.scalar.copy(out=dst, in_=src)
+
+        def bbc_mm(h):
+            bbc[h] = psum.tile([P, 512], F32, tag="bank", name="bbc%d" % h)
             nc.tensor.matmul(out=bbc[h][:], lhsT=sel_b[:], rhs=z[:, half(h)], start=True, stop=True)
+
+        def pn_mm(h):
             pn = psum.tile([P, 512], F32, tag="bank", name="pn%d" % h)
             nc.tensor.matmul(out=pn[:], lhsT=sel_n[:], rhs=z[:, half(h)], start=True, stop=True)
             nc.scalar.copy(out=posb[2][:, half(h)], in_=pn[:])
 
-        def make_posb(g, h):
-            nc.vector.tensor_tensor(out=posb[g][:, half(h)], in0=bbc[h][:], in1=pos_sb[g][:, half(h)], op=ADD)
+        def bbc_copy(h):
+            nc.scalar.copy(out=bbcs[:, half(h)], in_=bbc[h][:])
+
+        def make_posb(g, h, eng="V"):
+            if eng == "V":
+                nc.vector.tensor_tensor(out=posb[g][:, half(h)], in0=bbc[h][:], in1=pos_sb[g][:, half(h)], op=ADD)
+            else:
+                nc.gpsimd.tensor_tensor(out=posb[g][:, half(h)], in0=pos_sb[g][:, half(h)], in1=bbcs[:, half(h)], op=ADD)
 
         def regroup(c, j0, j1):
             nc.vector.tensor_copy(
@@ -102,26 +109,30 @@ def tile_tubeletembedding_kernel(tc, video, W, b, pos_embed, out):
                 in_=v_sb[:, c, :].rearrange("p (y j x) -> p j y x", j=6, x=16)[:, j0:j1, :, :],
             )
 
-        def tok_bank(r0, n, dst):
+        def tok_t(r0, n, dst, eng):
             pt = psum.tile([P, 512], F32, tag="bank", name="pt%d" % r0)
             for i in range(n):
                 r = r0 + i
                 nc.tensor.transpose(pt[:, i * P:(i + 1) * P], v2w[:, r * P:(r + 1) * P], perm1[:])
-            nc.scalar.copy(out=dst, in_=pt[:, 0:n * P].rearrange("p (r x t) -> p x r t", r=n, t=2))
+            copy_out(eng, dst, pt[:, 0:n * P].rearrange("p (r x t) -> p x r t", r=n, t=2))
 
-        def tok_group_bank(g, q):
+        def tok_bank(r0, n, eng="S"):
+            tok_t(r0, n, grpw[:, 0:256].rearrange("p (x r t) -> p x r t", r=2, t=2), eng)
+
+        def tok_group_bank(g, q, eng="S"):
             view = grpw[:, 256 + g * 1024:256 + (g + 1) * 1024].rearrange("p (x r t) -> p x r t", r=8, t=2)
-            tok_bank(2 + 8 * g + 4 * q, 4, view[:, :, 4 * q:4 * q + 4, :])
+            tok_t(2 + 8 * g + 4 * q, 4, view[:, :, 4 * q:4 * q + 4, :], eng)
 
-        def w_bank(h, q):
+        def w_bank(h, q, eng="S"):
             a0 = 4 * h + 2 * q
             pt = psum.tile([P, 512], F32, tag="bank", name="pw%d" % a0)
             for i in range(4):
                 a, u = a0 + i // 2, i % 2
                 nc.tensor.transpose(pt[:, i * P:(i + 1) * P], w_w[:, a * 256 + u * P:a * 256 + (u + 1) * P], ident[:])
-            nc.scalar.copy(
-                out=gww[:, a0 * 256:(a0 + 2) * 256].rearrange("p (a e u) -> p a e u", a=2, u=2),
-                in_=pt[:].rearrange("p (a u e) -> p a e u", a=2, u=2),
+            copy_out(
+                eng,
+                gww[:, a0 * 256:(a0 + 2) * 256].rearrange("p (a e u) -> p a e u", a=2, u=2),
+                pt[:].rearrange("p (a u e) -> p a e u", a=2, u=2),
             )
 
         def quant_tok(c0, n):
@@ -161,64 +172,83 @@ def tile_tubeletembedding_kernel(tc, video, W, b, pos_embed, out):
             cols = slice(0, 1024) if h is None else half(h)
             nc.sync.dma_start(out=dram(t, cols), in_=o_sb[t][:, cols])
 
-        w_bank(0, 0)
-        w_bank(0, 1)
-        bias_mm(0)
         regroup(0, 0, 2)
+        tok_bank(0, 2)
         regroup(0, 2, 6)
-        tok_bank(0, 2, grpw[:, 0:256].rearrange("p (x r t) -> p x r t", r=2, t=2))
-        tok_group_bank(0, 0)
-        regroup(1, 0, 4)
-        quant_w(0)
-        tok_group_bank(0, 1)
-        quant_tok(0, 128)
-        make_posb(0, 0)
-        mx(0, 0)
-        bias_mm(1)
-        w_bank(1, 0)
-        w_bank(1, 1)
-        add_v(0, 0)
-        store(0, 0)
-        quant_tok(128, 512)
-        regroup(1, 4, 6)
         regroup(2, 0, 6)
-        for t in (1, 2, 3, 4):
-            mx(t, 0)
-        tok_group_bank(1, 0)
+        tok_group_bank(0, 0)
+        quant_tok(0, 128)
+        regroup(1, 4, 6)
+        regroup(1, 0, 4)
+        w_bank(0, 1)
+        w_bank(0, 0)
+        bbc_mm(1)
+        bbc_copy(1)
+        quant_w(0)
+        pn_mm(0)
+        make_posb(0, 1, "G")
+        bbc_mm(0)
+        make_posb(0, 0)
+        tok_group_bank(0, 1)
         tok_group_bank(1, 1)
-        add_v(1, 0)
-        store(1, 0)
-        add_v(2, 0)
-        store(2, 0)
-        quant_w(1)
-        make_posb(0, 1)
-        add_v(3, 0)
-        mx(3, 1)
-        add_sg(3, 1)
-        mx(0, 1)
+        mx(0, 0)
+        w_bank(1, 1)
+        quant_tok(128, 512)
+        w_bank(1, 0)
+        mx(4, 0)
+        make_posb(1, 1, "G")
+        add_v(0, 0)
+        mx(3, 0)
         add_v(4, 0)
+        mx(2, 0)
+        quant_w(1)
+        add_v(2, 0)
+        mx(1, 0)
+        add_sg(3, 0)
+        tok_group_bank(1, 0)
         mx(4, 1)
-        add_sg(4, 1)
+        add_v(4, 1)
+        mx(0, 1)
+        mx(1, 1)
+        store(0, 0)
+        store(4, 0)
+        mx(3, 1)
+        quant_tok(640, 512)
+        mx(5, 1)
+        add_sg(1, 0)
+        mx(7, 1)
+        add_sg(7, 1)
+        add_v(3, 1)
+        mx(5, 0)
+        mx(7, 0)
+        make_posb(1, 0)
+        mx(6, 0)
+        store(2, 0)
+        add_sg(5, 1)
+        add_v(1, 1)
+        mx(8, 0)
+        mx(2, 1)
+        add_v(5, 0)
+        store(3, 0)
+        mx(6, 1)
+        store(4, 1)
+        pn_mm(1)
+        store(3, 1)
+        add_v(2, 1)
+        store(1, 0)
+        store(1, 1)
+        store(5, 0)
+        store(7, 1)
+        store(2, 1)
+        add_v(7, 0)
+        store(7, 0)
         add_v(0, 1)
         store(0, 1)
-        mx(1, 1)
-        mx(2, 1)
-        quant_tok(640, 512)
-        add_v(1, 1)
-        store(1, 1)
-        add_v(2, 1)
-        store(2, 1)
-        store(3)
-        store(4)
-        make_posb(1, 0)
-        make_posb(1, 1)
-        for t in (5, 6, 7):
-            mx(t, 1)
-            add_sg(t, 1)
-            mx(t, 0)
-            add_v(t, 0)
-            store(t)
-        for h in range(2):
-            mx(8, h)
-            add_v(8, h)
-            store(8, h)
+        mx(8, 1)
+        add_sg(6, 1)
+        add_v(8, 1)
+        add_v(8, 0)
+        store(5, 1)
+        add_v(6, 0)
+        store(8)
+        store(6)

from contextlib import ExitStack

import concourse.mybir as mybir
from concourse.masks import make_identity

F32 = mybir.dt.float32
BF16 = mybir.dt.bfloat16
U32 = mybir.dt.uint32
U8 = mybir.dt.uint8
FP8X4 = mybir.dt.float8_e4m3fn_x4
ADD = mybir.AluOpType.add
P = 128
FLOPS = 2 * 1152 * 512 * 1024


def tile_tubeletembedding_kernel(tc, video, W, b, pos_embed, out):
    nc = tc.nc
    with ExitStack() as ctx:
        keep = ctx.enter_context(tc.tile_pool(name="keep", bufs=1))
        psum = ctx.enter_context(tc.psum_pool(name="psum", bufs=8))
        ctx.enter_context(tc.manual_schedule())

        vid = video.rearrange("b t o (h c y) x -> (b t o h) c (y x)", h=2, c=3, y=16)
        wv = W.rearrange("(a p) k -> p a k", p=P)
        pv = pos_embed.rearrange("o (s r) e -> (o s) r e", r=18)
        ov = out.rearrange("b (s r) e -> b s r e", r=18)
        on = out.rearrange("b (s r) e -> (b s) r e", r=18)

        ident = keep.tile([P, P], F32)
        make_identity(nc, ident[:])
        z = keep.tile([P, 1024], BF16)
        nc.vector.memset(z[:], 0.0)

        v_sb = keep.tile([P, 3, 1536], BF16)
        w_sb = keep.tile([P, 8, 512], BF16)
        pos_sb = [keep.tile([P, 1024], BF16, name="pos%d" % g) for g in range(2)]
        nc.sync.dma_start(out=v_sb[:, 0, :], in_=vid[:, 0, :])
        nc.sync.dma_start(out=w_sb[:, 0:4, :], in_=wv[:, 0:4, :])
        nc.sync.dma_start(out=z[32:33, :], in_=b.unsqueeze(0))
        nc.sync.dma_start(out=v_sb[:, 2, :], in_=vid[:, 2, :])
        nc.sync.dma_start(out=z[0:32, :], in_=pv[:, 0:2, :])
        nc.sync.dma_start(out=v_sb[:, 1, :], in_=vid[:, 1, :])
        nc.sync.dma_start(out=pos_sb[1][:], in_=pv[:, 10:18, :])
        nc.sync.dma_start(out=pos_sb[0][:], in_=pv[:, 2:10, :])
        nc.sync.dma_start(out=w_sb[:, 4:8, :], in_=wv[:, 4:8, :])

        perm1 = keep.tile([P, P], F32)
        nc.vector.tensor_copy(
            out=perm1[:].rearrange("p (a h t) -> p a h t", h=2, t=2),
            in_=ident[:].rearrange("p (a t h) -> p a h t", t=2, h=2),
        )
        sel_n = keep.tile([P, P], BF16)
        nc.vector.tensor_tensor(
            out=sel_n[:].rearrange("p (c q) -> p c q", c=4),
            in0=ident[:, 0:32].unsqueeze(1).to_broadcast([P, 4, 32]),
            in1=ident[:, 32:33].unsqueeze(1).to_broadcast([P, 4, 32]),
            op=ADD,
        )
        sel_b = keep.tile([P, P], BF16)
        nc.vector.tensor_copy(out=sel_b[:], in_=ident[:, 32:33].to_broadcast([P, P]))

        v2 = keep.tile([P, 4608], BF16)
        v2w = v2[:].bitcast(F32)
        grp = keep.tile([P, 4608], BF16, align_bytes=64)
        grpw = grp[:].bitcast(F32)
        tokc = keep.tile([P, 1152], U32, align_bytes=64)
        toks = keep.tile([P, 1152], U8, align_bytes=64)
        gw = keep.tile([P, 4096], BF16, align_bytes=64)
        gww = gw[:].bitcast(F32)
        wc = keep.tile([P, 1024], U32, align_bytes=64)
        ws = keep.tile([P, 1024], U8, align_bytes=64)
        w_w = w_sb[:].rearrange("p a k -> p (a k)").bitcast(F32)
        posb = [keep.tile([P, 1024], F32, name="posb%d" % g) for g in range(3)]
        o_sb = [keep.tile([P, 1024], F32, name="o%d" % t) for t in range(9)]
        bbcs = keep.tile([P, 1024], F32)
        bbc = {}
        accs = {}

        def half(h):
            return slice(h * 512, (h + 1) * 512)

        def copy_out(eng, dst, src):
            if eng == "V":
                nc.vector.tensor_copy(out=dst, in_=src)
            else:
                nc.scalar.copy(out=dst, in_=src)

        def bbc_mm(h):
            bbc[h] = psum.tile([P, 512], F32, tag="bank", name="bbc%d" % h)
            nc.tensor.matmul(out=bbc[h][:], lhsT=sel_b[:], rhs=z[:, half(h)], start=True, stop=True)

        def pn_mm(h):
            pn = psum.tile([P, 512], F32, tag="bank", name="pn%d" % h)
            nc.tensor.matmul(out=pn[:], lhsT=sel_n[:], rhs=z[:, half(h)], start=True, stop=True)
            nc.scalar.copy(out=posb[2][:, half(h)], in_=pn[:])

        def bbc_copy(h):
            nc.scalar.copy(out=bbcs[:, half(h)], in_=bbc[h][:])

        def make_posb(g, h, eng="V"):
            if eng == "V":
                nc.vector.tensor_tensor(out=posb[g][:, half(h)], in0=bbc[h][:], in1=pos_sb[g][:, half(h)], op=ADD)
            else:
                nc.gpsimd.tensor_tensor(out=posb[g][:, half(h)], in0=pos_sb[g][:, half(h)], in1=bbcs[:, half(h)], op=ADD)

        def regroup(c, j0, j1):
            nc.vector.tensor_copy(
                out=v2[:, c * 1536 + j0 * 256:c * 1536 + j1 * 256].rearrange("p (j y x) -> p j y x", y=16, x=16),
                in_=v_sb[:, c, :].rearrange("p (y j x) -> p j y x", j=6, x=16)[:, j0:j1, :, :],
            )

        def tok_t(r0, n, dst, eng):
            pt = psum.tile([P, 512], F32, tag="bank", name="pt%d" % r0)
            for i in range(n):
                r = r0 + i
                nc.tensor.transpose(pt[:, i * P:(i + 1) * P], v2w[:, r * P:(r + 1) * P], perm1[:])
            copy_out(eng, dst, pt[:, 0:n * P].rearrange("p (r x t) -> p x r t", r=n, t=2))

        def tok_bank(r0, n, eng="S"):
            tok_t(r0, n, grpw[:, 0:256].rearrange("p (x r t) -> p x r t", r=2, t=2), eng)

        def tok_group_bank(g, q, eng="S"):
            view = grpw[:, 256 + g * 1024:256 + (g + 1) * 1024].rearrange("p (x r t) -> p x r t", r=8, t=2)
            tok_t(2 + 8 * g + 4 * q, 4, view[:, :, 4 * q:4 * q + 4, :], eng)

        def w_bank(h, q, eng="S"):
            a0 = 4 * h + 2 * q
            pt = psum.tile([P, 512], F32, tag="bank", name="pw%d" % a0)
            for i in range(4):
                a, u = a0 + i // 2, i % 2
                nc.tensor.transpose(pt[:, i * P:(i + 1) * P], w_w[:, a * 256 + u * P:a * 256 + (u + 1) * P], ident[:])
            copy_out(
                eng,
                gww[:, a0 * 256:(a0 + 2) * 256].rearrange("p (a e u) -> p a e u", a=2, u=2),
                pt[:].rearrange("p (a u e) -> p a e u", a=2, u=2),
            )

        def quant_tok(c0, n):
            nc.vector.quantize_mx(out=tokc[:, c0:c0 + n].bitcast(FP8X4), scales=toks[:, c0:c0 + n], in_=grp[:, 4 * c0:4 * (c0 + n)])

        def quant_w(h):
            nc.vector.quantize_mx(out=wc[:, half(h)].bitcast(FP8X4), scales=ws[:, half(h)], in_=gw[:, h * 2048:(h + 1) * 2048])

        def mx(t, h):
            acc = psum.tile([P, 512], F32, tag="bank", name="acc%d_%d" % (t, h))
            nc.tensor.matmul_mx(
                out=acc[:],
                lhsT=tokc[:, t * P:(t + 1) * P].bitcast(FP8X4), lhsT_scale=toks[:, t * P:(t + 1) * P],
                rhs=wc[:, half(h)].bitcast(FP8X4), rhs_scale=ws[:, half(h)],
                start=True, stop=True,
            )
            accs[(t, h)] = acc

        def group_of(t):
            return 2 if t == 0 else (t - 1) // 4

        def add_v(t, h):
            nc.vector.tensor_tensor(out=o_sb[t][:, half(h)], in0=accs[(t, h)][:], in1=posb[group_of(t)][:, half(h)], op=ADD)

        def add_sg(t, h):
            tmp = keep.tile([P, 512], F32, name="tmp%d_%d" % (t, h))
            nc.scalar.copy(out=tmp[:], in_=accs[(t, h)][:])
            nc.gpsimd.tensor_tensor(out=o_sb[t][:, half(h)], in0=tmp[:], in1=posb[group_of(t)][:, half(h)], op=ADD)

        def dram(t, cols):
            if t == 0:
                return on[:, 0:2, cols]
            g, bi = (t - 1) // 4, (t - 1) % 4
            return ov[bi, :, 2 + 8 * g:10 + 8 * g, cols]

        def store(t, h=None):
            cols = slice(0, 1024) if h is None else half(h)
            nc.sync.dma_start(out=dram(t, cols), in_=o_sb[t][:, cols])

        regroup(0, 0, 2)
        tok_bank(0, 2)
        regroup(0, 2, 6)
        regroup(2, 0, 6)
        tok_group_bank(0, 0)
        quant_tok(0, 128)
        regroup(1, 4, 6)
        regroup(1, 0, 4)
        w_bank(0, 1)
        w_bank(0, 0)
        bbc_mm(1)
        bbc_copy(1)
        quant_w(0)
        pn_mm(0)
        make_posb(0, 1, "G")
        bbc_mm(0)
        make_posb(0, 0)
        tok_group_bank(0, 1)
        tok_group_bank(1, 1)
        mx(0, 0)
        w_bank(1, 1)
        quant_tok(128, 512)
        w_bank(1, 0)
        mx(4, 0)
        make_posb(1, 1, "G")
        add_v(0, 0)
        mx(3, 0)
        add_v(4, 0)
        mx(2, 0)
        quant_w(1)
        add_v(2, 0)
        mx(1, 0)
        add_sg(3, 0)
        tok_group_bank(1, 0)
        mx(4, 1)
        add_v(4, 1)
        mx(0, 1)
        mx(1, 1)
        store(0, 0)
        store(4, 0)
        mx(3, 1)
        quant_tok(640, 512)
        mx(5, 1)
        add_sg(1, 0)
        mx(7, 1)
        add_sg(7, 1)
        add_v(3, 1)
        mx(5, 0)
        mx(7, 0)
        make_posb(1, 0)
        mx(6, 0)
        store(2, 0)
        add_sg(5, 1)
        add_v(1, 1)
        mx(8, 0)
        mx(2, 1)
        add_v(5, 0)
        store(3, 0)
        mx(6, 1)
        store(4, 1)
        pn_mm(1)
        store(3, 1)
        add_v(2, 1)
        store(1, 0)
        store(1, 1)
        store(5, 0)
        store(7, 1)
        store(2, 1)
        add_v(7, 0)
        store(7, 0)
        add_v(0, 1)
        store(0, 1)
        mx(8, 1)
        add_sg(6, 1)
        add_v(8, 1)
        add_v(8, 0)
        store(5, 1)
        add_v(6, 0)
        store(8)
        store(6)
